import numpy as np
import ml_dtypes


def mxq(x, axis, fmt="e4m3"):
    dtype, down = {"e4m3": (ml_dtypes.float8_e4m3fn, 7), "e5m2": (ml_dtypes.float8_e5m2, 14)}[fmt]
    v = np.moveaxis(np.asarray(x, np.float32).astype(ml_dtypes.bfloat16).astype(np.float64), axis, -1)
    blocks = v.reshape(v.shape[:-1] + (-1, 32))
    amax = np.abs(blocks).max(-1, keepdims=True)
    byte = np.maximum(np.where(amax > 0, np.frexp(amax)[1] - 1 + 127, 0) - down, 1)
    scale = np.exp2(byte - 127.0)
    codes = (blocks / scale).astype(np.float32).astype(dtype).astype(np.float64)
    return np.moveaxis((codes * scale).reshape(v.shape), -1, axis)


WIDE = False


def mx_kscale(k):
    if not WIDE:
        return np.ones(k)
    levels = np.array([10, -10, 5, -5, 0])
    a = np.random.permutation(np.resize(levels, k // 512 * 4)).reshape(k // 512, 4)
    idx = np.arange(k)
    return np.exp2(a[idx // 512, idx % 128 // 32])


BF16 = ml_dtypes.bfloat16


def bf(x):
    return np.asarray(x, np.float32).astype(BF16)


def f64(x):
    return np.asarray(x).astype(np.float64)


E2M1 = np.array([0.0, 0.5, 1.0, 1.5, 2.0, 3.0, 4.0, 6.0, -0.0, -0.5, -1.0, -1.5, -2.0, -3.0, -4.0, -6.0])


def pack_weight(w, fmt):
    k, n = w.shape
    w = f64(bf(w)).reshape(k // 32, 32, n)
    amax = np.abs(w).max(1)
    if fmt == "e4m3":
        byte = np.frexp(amax)[1] - 1 + 127 - 7
    else:
        mant, ex = np.frexp(amax / 6.0)
        byte = np.where(mant > 0.5, ex, ex - 1) + 127
    byte = np.clip(np.where(amax > 0, byte, 1), 1, 254)
    scaled = (w * np.exp2(127.0 - byte)[:, None, :]).reshape(k, n).astype(np.float32)
    by_word = np.ascontiguousarray(scaled.reshape(k // 512, 128, 4, n).transpose(0, 1, 3, 2))
    if fmt == "e4m3":
        words = by_word.astype(ml_dtypes.float8_e4m3fn).view(np.uint8)
    else:
        c = by_word.astype(ml_dtypes.float4_e2m1fn).view(np.uint8) & 0xF
        words = c[..., 0::2] | (c[..., 1::2] << 4)
    return np.ascontiguousarray(words), np.ascontiguousarray(byte.astype(np.uint8).reshape(k // 512, 16, n))


def unpack_weight(words, scales, fmt):
    g, p, n, _ = words.shape
    if fmt == "e4m3":
        vals = np.ascontiguousarray(words).view(ml_dtypes.float8_e4m3fn).astype(np.float64)
    else:
        nib = np.empty((g, p, n, 4), np.uint8)
        nib[..., 0::2] = words & 0xF
        nib[..., 1::2] = words >> 4
        vals = E2M1[nib]
    vals = vals * np.repeat(np.exp2(scales.astype(np.float64) - 127.0), 8, axis=1)[..., None]
    return vals.transpose(0, 1, 3, 2).reshape(g * 512, n)

def pack4(w):
    words, scales = pack_weight(w, "e2m1")
    return words.reshape(words.shape[0], 128, -1), scales


def unpack4(words, scales):
    return unpack_weight(words.reshape(words.shape[0], 128, -1, 2), scales, "e2m1")


B, CB, CD, H, W = 4, 4, 512, 16, 16
C = CB * CD


def erf(z):
    z = np.clip(z, -6.0, 6.0)
    z2 = 2.0 * z * z
    term = z.copy()
    tot = z.copy()
    for n in range(1, 101):
        term *= z2
        term /= 2 * n + 1
        tot += term
    return 2.0 / np.sqrt(np.pi) * np.exp(-z * z) * tot


def gelu_erf(v):
    return 0.5 * v * (1.0 + erf(v / np.sqrt(2.0)))


def setup_inputs():
    s = mx_kscale(CD)
    s = s / s.max()
    sc = np.tile(s, CB)
    x = bf(np.random.standard_normal((B, C, H, W)) * sc[None, :, None, None])
    stack = np.random.standard_normal((CB, CD, CD)) / np.sqrt(CD) / s[None, :, None]
    words, scales = pack4(stack.reshape(-1, CD))
    return {"x": x, "wc_words": words, "wc_scales": scales}


def reference(x, wc_words, wc_scales):
    x = f64(x)
    xr = np.transpose(x, (0, 2, 3, 1)).reshape(B, H, W, CB, CD)
    xb = xr.transpose(3, 0, 1, 2, 4).reshape(CB, B * H * W, CD)
    out = mxq(xb, 2, "e4m3") @ unpack4(wc_words, wc_scales).reshape(CB, CD, CD)
    out = out.reshape(CB, B, H, W, CD).transpose(1, 2, 3, 0, 4)
    out = out.reshape(B, H, W, C).transpose(0, 3, 1, 2)
    return gelu_erf(x + out)

@@ -1,0 +1,162 @@
+from contextlib import ExitStack
+
+import concourse.mybir as mybir
+from concourse.masks import make_identity
+
+BF16 = mybir.dt.bfloat16
+F32 = mybir.dt.float32
+I32 = mybir.dt.int32
+U8 = mybir.dt.uint8
+U32 = mybir.dt.uint32
+FP8X4 = mybir.dt.float8_e4m3fn_x4
+FP4X4 = mybir.dt.float4_e2m1fn_x4
+
+P = 128
+PACK = 4
+BATCH = 4
+BLOCKS = 4
+CD = P * PACK
+HW = 256
+HALVES = HW // P
+QUADRANTS = 4
+
+FLOPS = 2 * BATCH * HW * BLOCKS * CD * CD
+
+
+def tile_spectralchannelmixing_e_kernel(tc, x, wc_words, wc_scales, out):
+    nc = tc.nc
+    x_view = x.rearrange("b (i p t) h w -> i b p (t h w)", i=BLOCKS, t=PACK)
+    out_view = out.rearrange("b (i p t) h w -> i b p (t h w)", i=BLOCKS, t=PACK)
+    rounds = [(i, b) for i in range(BLOCKS) for b in range(BATCH)]
+
+    with ExitStack() as ctx:
+        ctx.enter_context(tc.manual_schedule())
+        const = ctx.enter_context(tc.tile_pool(name="const", bufs=1))
+        inputs = ctx.enter_context(tc.tile_pool(name="inputs", bufs=len(rounds)))
+        stage = ctx.enter_context(tc.tile_pool(name="stage", bufs=4))
+        psum_xt = ctx.enter_context(tc.psum_pool(name="psum_xt", bufs=2))
+        psum_mix = ctx.enter_context(tc.psum_pool(name="psum_mix", bufs=3))
+        psum_sum = ctx.enter_context(tc.psum_pool(name="psum_sum", bufs=3))
+
+        scales = const.tile([P, BLOCKS, CD], U8, align_bytes=64)
+        nc.vector.memset(scales[:].bitcast(I32), 0)
+        zero = const.tile([P, 1], F32)
+        nc.vector.memset(zero[:], 0.0)
+        warm = const.tile([P, 1], F32)
+        nc.scalar.activation(out=warm[:], in_=zero[:], func=mybir.ActivationFunctionType.Gelu)
+        ident_bf16 = const.tile([P, P], BF16)
+        make_identity(nc, ident_bf16[:])
+        ident_f32 = const.tile([P, P], F32)
+        make_identity(nc, ident_f32[:])
+
+        words = const.tile([P, BLOCKS, 2 * CD], U8, align_bytes=64)
+        x_tiles = []
+        for r, (i, b) in enumerate(rounds):
+            x_tile = inputs.tile([P, PACK, HW], BF16, name="x_tile")
+            nc.sync.dma_start(out=x_tile[:].rearrange("p t s -> p (t s)"), in_=x_view[i, b])
+            x_tiles.append(x_tile)
+            if r == 0:
+                for quadrant in range(QUADRANTS):
+                    nc.sync.dma_start(
+                        out=scales[32 * quadrant : 32 * quadrant + 4, :, :].bitcast(I32),
+                        in_=wc_scales.bitcast(I32)[
+                            :, 4 * quadrant : 4 * quadrant + 4, :
+                        ].rearrange("g r n -> r g n"),
+                    )
+            if b == 0:
+                nc.sync.dma_start(
+                    out=words[:, i, :].bitcast(I32), in_=wc_words[i].bitcast(I32)
+                )
+
+        grouped, x_codes, x_scales = {}, {}, {}
+        xt_banks, xt = {}, {}
+        mix_banks, sums_t, sum_banks = {}, {}, {}
+
+        def regroup(r):
+            grouped[r] = stage.tile([P, HW, PACK], BF16, align_bytes=64, name="grouped")
+            nc.vector.tensor_copy(
+                out=grouped[r][:].rearrange("p (c k) t -> p c t k", k=4),
+                in_=x_tiles[r][:].rearrange("p t (c k) -> p c t k", k=4),
+            )
+
+        def quantise(r):
+            x_codes[r] = stage.tile([P, HW], U32, align_bytes=64, name="x_codes")
+            x_scales[r] = stage.tile([P, HW], U8, align_bytes=64, name="x_scales")
+            nc.vector.quantize_mx(
+                out=x_codes[r][:].bitcast(FP8X4),
+                scales=x_scales[r][:],
+                in_=grouped[r][:].rearrange("p s t -> p (s t)"),
+            )
+
+        def transpose_x(r):
+            xt_banks[r] = psum_xt.tile([P, HALVES, PACK, P], BF16, name="xt_bank")
+            for h in range(HALVES):
+                for t in range(PACK):
+                    nc.tensor.transpose(
+                        out=xt_banks[r][:, h, t, :],
+                        in_=x_tiles[r][:, t, P * h : P * (h + 1)],
+                        identity=ident_bf16[:],
+                    )
+
+        def copy_xt(r):
+            xt[r] = stage.tile([P, HALVES, PACK, P], BF16, name="xt")
+            nc.scalar.copy(out=xt[r][:], in_=xt_banks[r][:])
+
+        def multiply(r):
+            i = rounds[r][0]
+            for h in range(HALVES):
+                mix_banks[r, h] = psum_mix.tile([P, CD], F32, name="mix_bank")
+                nc.tensor.matmul_mx(
+                    out=mix_banks[r, h][:],
+                    lhsT=x_codes[r][:, P * h : P * (h + 1)].bitcast(FP8X4),
+                    lhsT_scale=x_scales[r][:, P * h : P * (h + 1)],
+                    rhs=words[:, i, :].bitcast(FP4X4),
+                    rhs_scale=scales[:, i, :],
+                    start=True,
+                    stop=True,
+                )
+
+        def add_residual(r):
+            sums_t[r] = stage.tile([P, HALVES, PACK, P], F32, name="sums_t")
+            for h in range(HALVES):
+                nc.vector.tensor_tensor(
+                    out=sums_t[r][:, h, :, :],
+                    in0=mix_banks[r, h][:].rearrange("s (p t) -> s t p", t=PACK),
+                    in1=xt[r][:, h, :, :],
+                    op=mybir.AluOpType.add,
+                )
+
+        def transpose_back(r):
+            for h in range(HALVES):
+                sum_banks[r, h] = psum_sum.tile([P, PACK, P], F32, name="sum_bank")
+                for t in range(PACK):
+                    nc.tensor.transpose(
+                        out=sum_banks[r, h][:, t, :],
+                        in_=sums_t[r][:, h, t, :],
+                        identity=ident_f32[:],
+                    )
+
+        def gelu_and_store(r):
+            i, b = rounds[r]
+            result = stage.tile([P, PACK, HW], F32, name="result")
+            for h in range(HALVES):
+                nc.scalar.activation(
+                    out=result[:, :, P * h : P * (h + 1)],
+                    in_=sum_banks[r, h][:],
+                    func=mybir.ActivationFunctionType.Gelu,
+                )
+            nc.sync.dma_start(out=out_view[i, b], in_=result[:].rearrange("p t s -> p (t s)"))
+
+        def at(r, stage_of_round):
+            if 0 <= r < len(rounds):
+                stage_of_round(r)
+
+        for k in range(-2, len(rounds) + 1):
+            at(k, multiply)
+            at(k - 1, transpose_back)
+            at(k + 2, transpose_x)
+            at(k, add_residual)
+            at(k + 1, quantise)
+            at(k + 2, regroup)
+            at(k - 1, gelu_and_store)
+            at(k + 2, copy_xt)

@@ -151,12 +151,12 @@ def tile_spectralchannelmixing_e_kernel(tc, x, wc_words, wc_scales, out):
             if 0 <= r < len(rounds):
                 stage_of_round(r)
 
-        for k in range(-2, len(rounds) + 1):
+        for k in range(-3, len(rounds) + 1):
             at(k, multiply)
             at(k - 1, transpose_back)
             at(k + 2, transpose_x)
             at(k, add_residual)
-            at(k + 1, quantise)
-            at(k + 2, regroup)
+            at(k + 2, quantise)
+            at(k + 3, regroup)
             at(k - 1, gelu_and_store)
             at(k + 2, copy_xt)

@@ -74,10 +74,15 @@ def tile_spectralchannelmixing_e_kernel(tc, x, wc_words, wc_scales, out):
 
         def regroup(r):
             grouped[r] = stage.tile([P, HW, PACK], BF16, align_bytes=64, name="grouped")
-            nc.vector.tensor_copy(
-                out=grouped[r][:].rearrange("p (c k) t -> p c t k", k=4),
-                in_=x_tiles[r][:].rearrange("p t (c k) -> p c t k", k=4),
-            )
+            for h in range(HALVES):
+                nc.gpsimd.tensor_scalar(
+                    out=grouped[r][:, P * h : P * (h + 1), :],
+                    in0=x_tiles[r][:, :, P * h : P * (h + 1)].rearrange("p t s -> p s t"),
+                    scalar1=1.0,
+                    scalar2=0.0,
+                    op0=mybir.AluOpType.mult,
+                    op1=mybir.AluOpType.add,
+                )
 
         def quantise(r):
             x_codes[r] = stage.tile([P, HW], U32, align_bytes=64, name="x_codes")

@@ -17,7 +17,8 @@ BATCH = 4
 BLOCKS = 4
 CD = P * PACK
 HW = 256
-HALVES = HW // P
+PARITIES = 2
+BANK_T = 2
 QUADRANTS = 4
 
 FLOPS = 2 * BATCH * HW * BLOCKS * CD * CD
@@ -44,10 +45,8 @@ def tile_spectralchannelmixing_e_kernel(tc, x, wc_words, wc_scales, out):
         nc.vector.memset(zero[:], 0.0)
         warm = const.tile([P, 1], F32)
         nc.scalar.activation(out=warm[:], in_=zero[:], func=mybir.ActivationFunctionType.Gelu)
-        ident_bf16 = const.tile([P, P], BF16)
-        make_identity(nc, ident_bf16[:])
-        ident_f32 = const.tile([P, P], F32)
-        make_identity(nc, ident_f32[:])
+        identity = const.tile([P, P], F32)
+        make_identity(nc, identity[:])
 
         words = const.tile([P, BLOCKS, 2 * CD], U8, align_bytes=64)
         x_tiles = []
@@ -73,11 +72,12 @@ def tile_spectralchannelmixing_e_kernel(tc, x, wc_words, wc_scales, out):
         mix_banks, sums_t, sum_banks = {}, {}, {}
 
         def regroup(r):
-            grouped[r] = stage.tile([P, HW, PACK], BF16, align_bytes=64, name="grouped")
-            for h in range(HALVES):
+            grouped[r] = stage.tile([P, PARITIES, P, PACK], BF16, align_bytes=64, name="grouped")
+            by_parity = x_tiles[r][:].rearrange("p t (u e) -> p e u t", e=PARITIES)
+            for e in range(PARITIES):
                 nc.gpsimd.tensor_scalar(
-                    out=grouped[r][:, P * h : P * (h + 1), :],
-                    in0=x_tiles[r][:, :, P * h : P * (h + 1)].rearrange("p t s -> p s t"),
+                    out=grouped[r][:, e, :, :],
+                    in0=by_parity[:, e, :, :],
                     scalar1=1.0,
                     scalar2=0.0,
                     op0=mybir.AluOpType.mult,
@@ -85,36 +85,38 @@ def tile_spectralchannelmixing_e_kernel(tc, x, wc_words, wc_scales, out):
                 )
 
         def quantise(r):
-            x_codes[r] = stage.tile([P, HW], U32, align_bytes=64, name="x_codes")
-            x_scales[r] = stage.tile([P, HW], U8, align_bytes=64, name="x_scales")
+            x_codes[r] = stage.tile([P, PARITIES, P], U32, align_bytes=64, name="x_codes")
+            x_scales[r] = stage.tile([P, PARITIES, P], U8, align_bytes=64, name="x_scales")
             nc.vector.quantize_mx(
-                out=x_codes[r][:].bitcast(FP8X4),
-                scales=x_scales[r][:],
-                in_=grouped[r][:].rearrange("p s t -> p (s t)"),
+                out=x_codes[r][:].rearrange("p e u -> p (e u)").bitcast(FP8X4),
+                scales=x_scales[r][:].rearrange("p e u -> p (e u)"),
+                in_=grouped[r][:].rearrange("p e u t -> p (e u t)"),
             )
 
         def transpose_x(r):
-            xt_banks[r] = psum_xt.tile([P, HALVES, PACK, P], BF16, name="xt_bank")
-            for h in range(HALVES):
-                for t in range(PACK):
-                    nc.tensor.transpose(
-                        out=xt_banks[r][:, h, t, :],
-                        in_=x_tiles[r][:, t, P * h : P * (h + 1)],
-                        identity=ident_bf16[:],
-                    )
+            xt_banks[r] = psum_xt.tile([P, PACK, P], F32, name="xt_bank")
+            for t in range(PACK):
+                nc.tensor.transpose(
+                    out=xt_banks[r][:, t, :],
+                    in_=x_tiles[r][:, t, :].bitcast(F32),
+                    identity=identity[:],
+                )
 
         def copy_xt(r):
-            xt[r] = stage.tile([P, HALVES, PACK, P], BF16, name="xt")
-            nc.scalar.copy(out=xt[r][:], in_=xt_banks[r][:])
+            xt[r] = stage.tile([P, PACK, P, PARITIES], BF16, name="xt")
+            nc.scalar.copy(
+                out=xt[r][:].rearrange("u t p e -> u (t p e)"),
+                in_=xt_banks[r][:].rearrange("u t p -> u (t p)").bitcast(BF16),
+            )
 
         def multiply(r):
             i = rounds[r][0]
-            for h in range(HALVES):
-                mix_banks[r, h] = psum_mix.tile([P, CD], F32, name="mix_bank")
+            for e in range(PARITIES):
+                mix_banks[r, e] = psum_mix.tile([P, CD], F32, name="mix_bank")
                 nc.tensor.matmul_mx(
-                    out=mix_banks[r, h][:],
-                    lhsT=x_codes[r][:, P * h : P * (h + 1)].bitcast(FP8X4),
-                    lhsT_scale=x_scales[r][:, P * h : P * (h + 1)],
+                    out=mix_banks[r, e][:],
+                    lhsT=x_codes[r][:, e, :].bitcast(FP8X4),
+                    lhsT_scale=x_scales[r][:, e, :],
                     rhs=words[:, i, :].bitcast(FP4X4),
                     rhs_scale=scales[:, i, :],
                     start=True,
@@ -122,35 +124,38 @@ def tile_spectralchannelmixing_e_kernel(tc, x, wc_words, wc_scales, out):
                 )
 
         def add_residual(r):
-            sums_t[r] = stage.tile([P, HALVES, PACK, P], F32, name="sums_t")
-            for h in range(HALVES):
+            sums_t[r] = stage.tile([P, PARITIES, PACK, P], F32, name="sums_t")
+            for e in range(PARITIES):
                 nc.vector.tensor_tensor(
-                    out=sums_t[r][:, h, :, :],
-                    in0=mix_banks[r, h][:].rearrange("s (p t) -> s t p", t=PACK),
-                    in1=xt[r][:, h, :, :],
+                    out=sums_t[r][:, e, :, :],
+                    in0=mix_banks[r, e][:].rearrange("u (p t) -> u t p", t=PACK),
+                    in1=xt[r][:, :, :, e],
                     op=mybir.AluOpType.add,
                 )
 
         def transpose_back(r):
-            for h in range(HALVES):
-                sum_banks[r, h] = psum_sum.tile([P, PACK, P], F32, name="sum_bank")
-                for t in range(PACK):
+            for t in range(PACK):
+                if t % BANK_T == 0:
+                    sum_banks[r, t // BANK_T] = psum_sum.tile(
+                        [P, BANK_T, PARITIES, P], F32, name="sum_bank"
+                    )
+                for e in range(PARITIES):
                     nc.tensor.transpose(
-                        out=sum_banks[r, h][:, t, :],
-                        in_=sums_t[r][:, h, t, :],
-                        identity=ident_f32[:],
+                        out=sum_banks[r, t // BANK_T][:, t % BANK_T, e, :],
+                        in_=sums_t[r][:, e, t, :],
+                        identity=identity[:],
                     )
 
         def gelu_and_store(r):
             i, b = rounds[r]
-            result = stage.tile([P, PACK, HW], F32, name="result")
-            for h in range(HALVES):
+            result = stage.tile([P, PACK, P, PARITIES], F32, name="result")
+            for bank in range(PACK // BANK_T):
                 nc.scalar.activation(
-                    out=result[:, :, P * h : P * (h + 1)],
-                    in_=sum_banks[r, h][:],
+                    out=result[:, BANK_T * bank : BANK_T * (bank + 1), :, :],
+                    in_=sum_banks[r, bank][:].rearrange("p t e u -> p t u e"),
                     func=mybir.ActivationFunctionType.Gelu,
                 )
-            nc.sync.dma_start(out=out_view[i, b], in_=result[:].rearrange("p t s -> p (t s)"))
+            nc.sync.dma_start(out=out_view[i, b], in_=result[:].rearrange("p t u e -> p (t u e)"))
 
         def at(r, stage_of_round):
             if 0 <= r < len(rounds):

@@ -17,8 +17,7 @@ BATCH = 4
 BLOCKS = 4
 CD = P * PACK
 HW = 256
-PARITIES = 2
-BANK_T = 2
+HALVES = HW // P
 QUADRANTS = 4
 
 FLOPS = 2 * BATCH * HW * BLOCKS * CD * CD
@@ -45,8 +44,10 @@ def tile_spectralchannelmixing_e_kernel(tc, x, wc_words, wc_scales, out):
         nc.vector.memset(zero[:], 0.0)
         warm = const.tile([P, 1], F32)
         nc.scalar.activation(out=warm[:], in_=zero[:], func=mybir.ActivationFunctionType.Gelu)
-        identity = const.tile([P, P], F32)
-        make_identity(nc, identity[:])
+        ident_bf16 = const.tile([P, P], BF16)
+        make_identity(nc, ident_bf16[:])
+        ident_f32 = const.tile([P, P], F32)
+        make_identity(nc, ident_f32[:])
 
         words = const.tile([P, BLOCKS, 2 * CD], U8, align_bytes=64)
         x_tiles = []
@@ -72,51 +73,52 @@ def tile_spectralchannelmixing_e_kernel(tc, x, wc_words, wc_scales, out):
         mix_banks, sums_t, sum_banks = {}, {}, {}
 
         def regroup(r):
-            grouped[r] = stage.tile([P, PARITIES, P, PACK], BF16, align_bytes=64, name="grouped")
-            by_parity = x_tiles[r][:].rearrange("p t (u e) -> p e u t", e=PARITIES)
-            for e in range(PARITIES):
-                nc.gpsimd.tensor_scalar(
-                    out=grouped[r][:, e, :, :],
-                    in0=by_parity[:, e, :, :],
-                    scalar1=1.0,
-                    scalar2=0.0,
-                    op0=mybir.AluOpType.mult,
-                    op1=mybir.AluOpType.add,
-                )
+            grouped[r] = stage.tile([P, HW, PACK], BF16, align_bytes=64, name="grouped")
+            nc.vector.tensor_copy(
+                out=grouped[r][:, 0:P, :].rearrange("p (c k) t -> p c t k", k=4),
+                in_=x_tiles[r][:, :, 0:P].rearrange("p t (c k) -> p c t k", k=4),
+            )
+            nc.gpsimd.tensor_scalar(
+                out=grouped[r][:, P:HW, :],
+                in0=x_tiles[r][:, :, P:HW].rearrange("p t s -> p s t"),
+                scalar1=1.0,
+                scalar2=0.0,
+                op0=mybir.AluOpType.mult,
+                op1=mybir.AluOpType.add,
+            )
 
         def quantise(r):
-            x_codes[r] = stage.tile([P, PARITIES, P], U32, align_bytes=64, name="x_codes")
-            x_scales[r] = stage.tile([P, PARITIES, P], U8, align_bytes=64, name="x_scales")
-            nc.vector.quantize_mx(
-                out=x_codes[r][:].rearrange("p e u -> p (e u)").bitcast(FP8X4),
-                scales=x_scales[r][:].rearrange("p e u -> p (e u)"),
-                in_=grouped[r][:].rearrange("p e u t -> p (e u t)"),
-            )
-
-        def transpose_x(r):
-            xt_banks[r] = psum_xt.tile([P, PACK, P], F32, name="xt_bank")
-            for t in range(PACK):
-                nc.tensor.transpose(
-                    out=xt_banks[r][:, t, :],
-                    in_=x_tiles[r][:, t, :].bitcast(F32),
-                    identity=identity[:],
+            x_codes[r] = stage.tile([P, HW], U32, align_bytes=64, name="x_codes")
+            x_scales[r] = stage.tile([P, HW], U8, align_bytes=64, name="x_scales")
+            for h in range(HALVES):
+                nc.vector.quantize_mx(
+                    out=x_codes[r][:, P * h : P * (h + 1)].bitcast(FP8X4),
+                    scales=x_scales[r][:, P * h : P * (h + 1)],
+                    in_=grouped[r][:, P * h : P * (h + 1), :].rearrange("p s t -> p (s t)"),
                 )
 
+        def transpose_x(r):
+            xt_banks[r] = psum_xt.tile([P, HALVES, PACK, P], BF16, name="xt_bank")
+            for h in range(HALVES):
+                for t in range(PACK):
+                    nc.tensor.transpose(
+                        out=xt_banks[r][:, h, t, :],
+                        in_=x_tiles[r][:, t, P * h : P * (h + 1)],
+                        identity=ident_bf16[:],
+                    )
+
         def copy_xt(r):
-            xt[r] = stage.tile([P, PACK, P, PARITIES], BF16, name="xt")
-            nc.scalar.copy(
-                out=xt[r][:].rearrange("u t p e -> u (t p e)"),
-                in_=xt_banks[r][:].rearrange("u t p -> u (t p)").bitcast(BF16),
-            )
+            xt[r] = stage.tile([P, HALVES, PACK, P], BF16, name="xt")
+            nc.scalar.copy(out=xt[r][:], in_=xt_banks[r][:])
 
         def multiply(r):
             i = rounds[r][0]
-            for e in range(PARITIES):
-                mix_banks[r, e] = psum_mix.tile([P, CD], F32, name="mix_bank")
+            for h in range(HALVES):
+                mix_banks[r, h] = psum_mix.tile([P, CD], F32, name="mix_bank")
                 nc.tensor.matmul_mx(
-                    out=mix_banks[r, e][:],
-                    lhsT=x_codes[r][:, e, :].bitcast(FP8X4),
-                    lhsT_scale=x_scales[r][:, e, :],
+                    out=mix_banks[r, h][:],
+                    lhsT=x_codes[r][:, P * h : P * (h + 1)].bitcast(FP8X4),
+                    lhsT_scale=x_scales[r][:, P * h : P * (h + 1)],
                     rhs=words[:, i, :].bitcast(FP4X4),
                     rhs_scale=scales[:, i, :],
                     start=True,
@@ -124,38 +126,35 @@ def tile_spectralchannelmixing_e_kernel(tc, x, wc_words, wc_scales, out):
                 )
 
         def add_residual(r):
-            sums_t[r] = stage.tile([P, PARITIES, PACK, P], F32, name="sums_t")
-            for e in range(PARITIES):
+            sums_t[r] = stage.tile([P, HALVES, PACK, P], F32, name="sums_t")
+            for h in range(HALVES):
                 nc.vector.tensor_tensor(
-                    out=sums_t[r][:, e, :, :],
-                    in0=mix_banks[r, e][:].rearrange("u (p t) -> u t p", t=PACK),
-                    in1=xt[r][:, :, :, e],
+                    out=sums_t[r][:, h, :, :],
+                    in0=mix_banks[r, h][:].rearrange("s (p t) -> s t p", t=PACK),
+                    in1=xt[r][:, h, :, :],
                     op=mybir.AluOpType.add,
                 )
 
         def transpose_back(r):
-            for t in range(PACK):
-                if t % BANK_T == 0:
-                    sum_banks[r, t // BANK_T] = psum_sum.tile(
-                        [P, BANK_T, PARITIES, P], F32, name="sum_bank"
-                    )
-                for e in range(PARITIES):
+            for h in range(HALVES):
+                sum_banks[r, h] = psum_sum.tile([P, PACK, P], F32, name="sum_bank")
+                for t in range(PACK):
                     nc.tensor.transpose(
-                        out=sum_banks[r, t // BANK_T][:, t % BANK_T, e, :],
-                        in_=sums_t[r][:, e, t, :],
-                        identity=identity[:],
+                        out=sum_banks[r, h][:, t, :],
+                        in_=sums_t[r][:, h, t, :],
+                        identity=ident_f32[:],
                     )
 
         def gelu_and_store(r):
             i, b = rounds[r]
-            result = stage.tile([P, PACK, P, PARITIES], F32, name="result")
-            for bank in range(PACK // BANK_T):
+            result = stage.tile([P, PACK, HW], F32, name="result")
+            for h in range(HALVES):
                 nc.scalar.activation(
-                    out=result[:, BANK_T * bank : BANK_T * (bank + 1), :, :],
-                    in_=sum_banks[r, bank][:].rearrange("p t e u -> p t u e"),
+                    out=result[:, :, P * h : P * (h + 1)],
+                    in_=sum_banks[r, h][:],
                     func=mybir.ActivationFunctionType.Gelu,
                 )
-            nc.sync.dma_start(out=out_view[i, b], in_=result[:].rearrange("p t u e -> p (t u e)"))
+            nc.sync.dma_start(out=out_view[i, b], in_=result[:].rearrange("p t s -> p (t s)"))
 
         def at(r, stage_of_round):
             if 0 <= r < len(rounds):

@@ -1,7 +1,6 @@
 from contextlib import ExitStack
 
 import concourse.mybir as mybir
-from concourse.masks import make_identity
 
 BF16 = mybir.dt.bfloat16
 F32 = mybir.dt.float32
@@ -17,8 +16,8 @@ BATCH = 4
 BLOCKS = 4
 CD = P * PACK
 HW = 256
-HALVES = HW // P
 QUADRANTS = 4
+GP_POS = 192
 
 FLOPS = 2 * BATCH * HW * BLOCKS * CD * CD
 
@@ -34,124 +33,108 @@ def tile_spectralchannelmixing_e_kernel(tc, x, wc_words, wc_scales, out):
         const = ctx.enter_context(tc.tile_pool(name="const", bufs=1))
         inputs = ctx.enter_context(tc.tile_pool(name="inputs", bufs=len(rounds)))
         stage = ctx.enter_context(tc.tile_pool(name="stage", bufs=4))
-        psum_xt = ctx.enter_context(tc.psum_pool(name="psum_xt", bufs=2))
-        psum_mix = ctx.enter_context(tc.psum_pool(name="psum_mix", bufs=3))
-        psum_sum = ctx.enter_context(tc.psum_pool(name="psum_sum", bufs=3))
+        results = ctx.enter_context(tc.tile_pool(name="results", bufs=6))
+        psum = ctx.enter_context(tc.psum_pool(name="psum", bufs=8))
 
-        scales = const.tile([P, BLOCKS, CD], U8, align_bytes=64)
-        nc.vector.memset(scales[:].bitcast(I32), 0)
+        scales_raw = const.tile([P, BLOCKS, CD], U8, align_bytes=64)
+        nc.vector.memset(scales_raw[:].bitcast(I32), 0)
         zero = const.tile([P, 1], F32)
         nc.vector.memset(zero[:], 0.0)
         warm = const.tile([P, 1], F32)
         nc.scalar.activation(out=warm[:], in_=zero[:], func=mybir.ActivationFunctionType.Gelu)
-        ident_bf16 = const.tile([P, P], BF16)
-        make_identity(nc, ident_bf16[:])
-        ident_f32 = const.tile([P, P], F32)
-        make_identity(nc, ident_f32[:])
 
-        words = const.tile([P, BLOCKS, 2 * CD], U8, align_bytes=64)
+        words_raw = const.tile([P, BLOCKS, 2 * CD], U8, align_bytes=64)
         x_tiles = []
         for r, (i, b) in enumerate(rounds):
+            if b == 0:
+                nc.sync.dma_start(
+                    out=words_raw[:, i, :].bitcast(I32), in_=wc_words[i].bitcast(I32)
+                )
             x_tile = inputs.tile([P, PACK, HW], BF16, name="x_tile")
             nc.sync.dma_start(out=x_tile[:].rearrange("p t s -> p (t s)"), in_=x_view[i, b])
             x_tiles.append(x_tile)
             if r == 0:
                 for quadrant in range(QUADRANTS):
                     nc.sync.dma_start(
-                        out=scales[32 * quadrant : 32 * quadrant + 4, :, :].bitcast(I32),
+                        out=scales_raw[32 * quadrant : 32 * quadrant + 4, :, :].bitcast(I32),
                         in_=wc_scales.bitcast(I32)[
                             :, 4 * quadrant : 4 * quadrant + 4, :
                         ].rearrange("g r n -> r g n"),
                     )
-            if b == 0:
-                nc.sync.dma_start(
-                    out=words[:, i, :].bitcast(I32), in_=wc_words[i].bitcast(I32)
-                )
+
+        words_sorted = const.tile([P, BLOCKS, PACK, 2 * P], U8, align_bytes=64)
+        scales_sorted = const.tile([P, BLOCKS, PACK, P], U8, align_bytes=64)
+
+        def sort_weight(i):
+            nc.vector.tensor_copy(
+                out=words_sorted[:, i, :, :].rearrange("p t (m e) -> p t m e", e=2),
+                in_=words_raw[:, i, :].rearrange("p (m t e) -> p t m e", t=PACK, e=2),
+            )
+            nc.vector.tensor_copy(
+                out=scales_sorted[:, i, :, :],
+                in_=scales_raw[:, i, :].rearrange("p (m t) -> p t m", t=PACK),
+            )
 
         grouped, x_codes, x_scales = {}, {}, {}
-        xt_banks, xt = {}, {}
-        mix_banks, sums_t, sum_banks = {}, {}, {}
+        banks, sums = {}, {}
 
         def regroup(r):
             grouped[r] = stage.tile([P, HW, PACK], BF16, align_bytes=64, name="grouped")
-            nc.vector.tensor_copy(
-                out=grouped[r][:, 0:P, :].rearrange("p (c k) t -> p c t k", k=4),
-                in_=x_tiles[r][:, :, 0:P].rearrange("p t (c k) -> p c t k", k=4),
-            )
             nc.gpsimd.tensor_scalar(
-                out=grouped[r][:, P:HW, :],
-                in0=x_tiles[r][:, :, P:HW].rearrange("p t s -> p s t"),
+                out=grouped[r][:, 0:GP_POS, :],
+                in0=x_tiles[r][:, :, 0:GP_POS].rearrange("p t s -> p s t"),
                 scalar1=1.0,
                 scalar2=0.0,
                 op0=mybir.AluOpType.mult,
                 op1=mybir.AluOpType.add,
             )
+            nc.scalar.copy(
+                out=grouped[r][:, GP_POS:HW, :],
+                in_=x_tiles[r][:, :, GP_POS:HW].rearrange("p t s -> p s t"),
+            )
 
         def quantise(r):
             x_codes[r] = stage.tile([P, HW], U32, align_bytes=64, name="x_codes")
             x_scales[r] = stage.tile([P, HW], U8, align_bytes=64, name="x_scales")
-            for h in range(HALVES):
-                nc.vector.quantize_mx(
-                    out=x_codes[r][:, P * h : P * (h + 1)].bitcast(FP8X4),
-                    scales=x_scales[r][:, P * h : P * (h + 1)],
-                    in_=grouped[r][:, P * h : P * (h + 1), :].rearrange("p s t -> p (s t)"),
-                )
-
-        def transpose_x(r):
-            xt_banks[r] = psum_xt.tile([P, HALVES, PACK, P], BF16, name="xt_bank")
-            for h in range(HALVES):
-                for t in range(PACK):
-                    nc.tensor.transpose(
-                        out=xt_banks[r][:, h, t, :],
-                        in_=x_tiles[r][:, t, P * h : P * (h + 1)],
-                        identity=ident_bf16[:],
-                    )
-
-        def copy_xt(r):
-            xt[r] = stage.tile([P, HALVES, PACK, P], BF16, name="xt")
-            nc.scalar.copy(out=xt[r][:], in_=xt_banks[r][:])
+            nc.vector.quantize_mx(
+                out=x_codes[r][:].bitcast(FP8X4),
+                scales=x_scales[r][:],
+                in_=grouped[r][:].rearrange("p s t -> p (s t)"),
+            )
 
         def multiply(r):
             i = rounds[r][0]
-            for h in range(HALVES):
-                mix_banks[r, h] = psum_mix.tile([P, CD], F32, name="mix_bank")
-                nc.tensor.matmul_mx(
-                    out=mix_banks[r, h][:],
-                    lhsT=x_codes[r][:, P * h : P * (h + 1)].bitcast(FP8X4),
-                    lhsT_scale=x_scales[r][:, P * h : P * (h + 1)],
-                    rhs=words[:, i, :].bitcast(FP4X4),
-                    rhs_scale=scales[:, i, :],
-                    start=True,
-                    stop=True,
-                )
+            for h in range(2):
+                banks[r, h] = psum.tile([P, 2, HW], F32, name="bank")
+                for e in range(2):
+                    t = 2 * h + e
+                    nc.tensor.matmul_mx(
+                        out=banks[r, h][:, e, :],
+                        lhsT=words_sorted[:, i, t, :].bitcast(FP4X4),
+                        lhsT_scale=scales_sorted[:, i, t, :],
+                        rhs=x_codes[r][:].bitcast(FP8X4),
+                        rhs_scale=x_scales[r][:],
+                        start=True,
+                        stop=True,
+                    )
 
         def add_residual(r):
-            sums_t[r] = stage.tile([P, HALVES, PACK, P], F32, name="sums_t")
-            for h in range(HALVES):
+            sums[r] = stage.tile([P, PACK, HW], F32, name="sums")
+            for h in range(2):
                 nc.vector.tensor_tensor(
-                    out=sums_t[r][:, h, :, :],
-                    in0=mix_banks[r, h][:].rearrange("s (p t) -> s t p", t=PACK),
-                    in1=xt[r][:, h, :, :],
+                    out=sums[r][:, 2 * h : 2 * h + 2, :],
+                    in0=banks[r, h][:],
+                    in1=x_tiles[r][:, 2 * h : 2 * h + 2, :],
                     op=mybir.AluOpType.add,
                 )
 
-        def transpose_back(r):
-            for h in range(HALVES):
-                sum_banks[r, h] = psum_sum.tile([P, PACK, P], F32, name="sum_bank")
-                for t in range(PACK):
-                    nc.tensor.transpose(
-                        out=sum_banks[r, h][:, t, :],
-                        in_=sums_t[r][:, h, t, :],
-                        identity=ident_f32[:],
-                    )
-
         def gelu_and_store(r):
             i, b = rounds[r]
-            result = stage.tile([P, PACK, HW], F32, name="result")
-            for h in range(HALVES):
+            result = results.tile([P, PACK, HW], F32, name="result")
+            for h in range(2):
                 nc.scalar.activation(
-                    out=result[:, :, P * h : P * (h + 1)],
-                    in_=sum_banks[r, h][:],
+                    out=result[:, 2 * h : 2 * h + 2, :],
+                    in_=sums[r][:, 2 * h : 2 * h + 2, :],
                     func=mybir.ActivationFunctionType.Gelu,
                 )
             nc.sync.dma_start(out=out_view[i, b], in_=result[:].rearrange("p t s -> p (t s)"))
@@ -160,12 +143,12 @@ def tile_spectralchannelmixing_e_kernel(tc, x, wc_words, wc_scales, out):
             if 0 <= r < len(rounds):
                 stage_of_round(r)
 
+        sort_weight(0)
         for k in range(-3, len(rounds) + 1):
             at(k, multiply)
-            at(k - 1, transpose_back)
-            at(k + 2, transpose_x)
+            at(k + 1, quantise)
             at(k, add_residual)
-            at(k + 2, quantise)
-            at(k + 3, regroup)
+            if k >= 0 and k % BATCH == 1 and k // BATCH + 1 < BLOCKS:
+                sort_weight(k // BATCH + 1)
             at(k - 1, gelu_and_store)
-            at(k + 2, copy_xt)
+            at(k + 3, regroup)

@@ -1,6 +1,7 @@
 from contextlib import ExitStack
 
 import concourse.mybir as mybir
+from concourse.masks import make_identity
 
 BF16 = mybir.dt.bfloat16
 F32 = mybir.dt.float32
@@ -34,7 +35,8 @@ def tile_spectralchannelmixing_e_kernel(tc, x, wc_words, wc_scales, out):
         inputs = ctx.enter_context(tc.tile_pool(name="inputs", bufs=len(rounds)))
         stage = ctx.enter_context(tc.tile_pool(name="stage", bufs=4))
         results = ctx.enter_context(tc.tile_pool(name="results", bufs=6))
-        psum = ctx.enter_context(tc.psum_pool(name="psum", bufs=8))
+        psum = ctx.enter_context(tc.psum_pool(name="psum", bufs=6))
+        psum_grp = ctx.enter_context(tc.psum_pool(name="psum_grp", bufs=2))
 
         scales_raw = const.tile([P, BLOCKS, CD], U8, align_bytes=64)
         nc.vector.memset(scales_raw[:].bitcast(I32), 0)
@@ -42,6 +44,9 @@ def tile_spectralchannelmixing_e_kernel(tc, x, wc_words, wc_scales, out):
         nc.vector.memset(zero[:], 0.0)
         warm = const.tile([P, 1], F32)
         nc.scalar.activation(out=warm[:], in_=zero[:], func=mybir.ActivationFunctionType.Gelu)
+
+        ident = const.tile([P, P], BF16)
+        make_identity(nc, ident[:])
 
         words_raw = const.tile([P, BLOCKS, 2 * CD], U8, align_bytes=64)
         x_tiles = []
@@ -88,10 +93,15 @@ def tile_spectralchannelmixing_e_kernel(tc, x, wc_words, wc_scales, out):
                 op0=mybir.AluOpType.mult,
                 op1=mybir.AluOpType.add,
             )
-            nc.scalar.copy(
-                out=grouped[r][:, GP_POS:HW, :],
-                in_=x_tiles[r][:, :, GP_POS:HW].rearrange("p t s -> p s t"),
+            grp_bank = psum_grp.tile([P, HW - GP_POS, PACK], BF16, name="grp_bank")
+            nc.tensor.matmul(
+                out=grp_bank[:],
+                lhsT=ident[:],
+                rhs=x_tiles[r][:, :, GP_POS:HW].rearrange("p t s -> p s t"),
+                start=True,
+                stop=True,
             )
+            nc.scalar.copy(out=grouped[r][:, GP_POS:HW, :], in_=grp_bank[:])
 
         def quantise(r):
             x_codes[r] = stage.tile([P, HW], U32, align_bytes=64, name="x_codes")

@@ -19,6 +19,8 @@ CD = P * PACK
 HW = 256
 QUADRANTS = 4
 GP_POS = 192
+HEAD_ROUNDS = 2
+HEAD_COPY_POS = 128
 
 FLOPS = 2 * BATCH * HW * BLOCKS * CD * CD
 
@@ -50,11 +52,9 @@ def tile_spectralchannelmixing_e_kernel(tc, x, wc_words, wc_scales, out):
 
         words_raw = const.tile([P, BLOCKS, 2 * CD], U8, align_bytes=64)
         x_tiles = []
+        for i in range(BLOCKS):
+            nc.sync.dma_start(out=words_raw[:, i, :].bitcast(I32), in_=wc_words[i].bitcast(I32))
         for r, (i, b) in enumerate(rounds):
-            if b == 0:
-                nc.sync.dma_start(
-                    out=words_raw[:, i, :].bitcast(I32), in_=wc_words[i].bitcast(I32)
-                )
             x_tile = inputs.tile([P, PACK, HW], BF16, name="x_tile")
             nc.sync.dma_start(out=x_tile[:].rearrange("p t s -> p (t s)"), in_=x_view[i, b])
             x_tiles.append(x_tile)
@@ -70,11 +70,13 @@ def tile_spectralchannelmixing_e_kernel(tc, x, wc_words, wc_scales, out):
         words_sorted = const.tile([P, BLOCKS, PACK, 2 * P], U8, align_bytes=64)
         scales_sorted = const.tile([P, BLOCKS, PACK, P], U8, align_bytes=64)
 
-        def sort_weight(i):
+        def sort_words(i):
             nc.vector.tensor_copy(
                 out=words_sorted[:, i, :, :].rearrange("p t (m e) -> p t m e", e=2),
                 in_=words_raw[:, i, :].rearrange("p (m t e) -> p t m e", t=PACK, e=2),
             )
+
+        def sort_scales(i):
             nc.vector.tensor_copy(
                 out=scales_sorted[:, i, :, :],
                 in_=scales_raw[:, i, :].rearrange("p (m t) -> p t m", t=PACK),
@@ -85,23 +87,31 @@ def tile_spectralchannelmixing_e_kernel(tc, x, wc_words, wc_scales, out):
 
         def regroup(r):
             grouped[r] = stage.tile([P, HW, PACK], BF16, align_bytes=64, name="grouped")
-            nc.gpsimd.tensor_scalar(
-                out=grouped[r][:, 0:GP_POS, :],
-                in0=x_tiles[r][:, :, 0:GP_POS].rearrange("p t s -> p s t"),
-                scalar1=1.0,
-                scalar2=0.0,
-                op0=mybir.AluOpType.mult,
-                op1=mybir.AluOpType.add,
-            )
-            grp_bank = psum_grp.tile([P, HW - GP_POS, PACK], BF16, name="grp_bank")
+            head = r < HEAD_ROUNDS
+            first = HEAD_COPY_POS if head else GP_POS
+            if head:
+                nc.scalar.copy(
+                    out=grouped[r][:, 0:first, :],
+                    in_=x_tiles[r][:, :, 0:first].rearrange("p t s -> p s t"),
+                )
+            else:
+                nc.gpsimd.tensor_scalar(
+                    out=grouped[r][:, 0:first, :],
+                    in0=x_tiles[r][:, :, 0:first].rearrange("p t s -> p s t"),
+                    scalar1=1.0,
+                    scalar2=0.0,
+                    op0=mybir.AluOpType.mult,
+                    op1=mybir.AluOpType.add,
+                )
+            grp_bank = psum_grp.tile([P, HW - first, PACK], BF16, name="grp_bank")
             nc.tensor.matmul(
                 out=grp_bank[:],
                 lhsT=ident[:],
-                rhs=x_tiles[r][:, :, GP_POS:HW].rearrange("p t s -> p s t"),
+                rhs=x_tiles[r][:, :, first:HW].rearrange("p t s -> p s t"),
                 start=True,
                 stop=True,
             )
-            nc.scalar.copy(out=grouped[r][:, GP_POS:HW, :], in_=grp_bank[:])
+            nc.scalar.copy(out=grouped[r][:, first:HW, :], in_=grp_bank[:])
 
         def quantise(r):
             x_codes[r] = stage.tile([P, HW], U32, align_bytes=64, name="x_codes")
@@ -153,12 +163,14 @@ def tile_spectralchannelmixing_e_kernel(tc, x, wc_words, wc_scales, out):
             if 0 <= r < len(rounds):
                 stage_of_round(r)
 
-        sort_weight(0)
+        for i in range(BLOCKS):
+            sort_words(i)
+        sort_scales(0)
         for k in range(-3, len(rounds) + 1):
             at(k, multiply)
             at(k + 1, quantise)
             at(k, add_residual)
             if k >= 0 and k % BATCH == 1 and k // BATCH + 1 < BLOCKS:
-                sort_weight(k // BATCH + 1)
+                sort_scales(k // BATCH + 1)
             at(k - 1, gelu_and_store)
             at(k + 3, regroup)

@@ -34,7 +34,6 @@ def tile_spectralchannelmixing_e_kernel(tc, x, wc_words, wc_scales, out):
     with ExitStack() as ctx:
         ctx.enter_context(tc.manual_schedule())
         const = ctx.enter_context(tc.tile_pool(name="const", bufs=1))
-        inputs = ctx.enter_context(tc.tile_pool(name="inputs", bufs=len(rounds)))
         stage = ctx.enter_context(tc.tile_pool(name="stage", bufs=4))
         results = ctx.enter_context(tc.tile_pool(name="results", bufs=6))
         psum = ctx.enter_context(tc.psum_pool(name="psum", bufs=6))
@@ -52,12 +51,22 @@ def tile_spectralchannelmixing_e_kernel(tc, x, wc_words, wc_scales, out):
 
         words_raw = const.tile([P, BLOCKS, 2 * CD], U8, align_bytes=64)
         x_tiles = []
-        for i in range(BLOCKS):
-            nc.sync.dma_start(out=words_raw[:, i, :].bitcast(I32), in_=wc_words[i].bitcast(I32))
+        nc.sync.dma_start(
+            out=words_raw[:].bitcast(I32), in_=wc_words.bitcast(I32).rearrange("g p n -> p g n")
+        )
         for r, (i, b) in enumerate(rounds):
-            x_tile = inputs.tile([P, PACK, HW], BF16, name="x_tile")
-            nc.sync.dma_start(out=x_tile[:].rearrange("p t s -> p (t s)"), in_=x_view[i, b])
-            x_tiles.append(x_tile)
+            if r < 2:
+                images = 1
+            elif r % 2 == 0:
+                images = 2
+            else:
+                continue
+            x_tile = const.tile([P, images, PACK, HW], BF16, name="x_tile%d" % r)
+            nc.sync.dma_start(
+                out=x_tile[:].rearrange("p b t s -> p b (t s)"),
+                in_=x_view[i, b : b + images].rearrange("b p n -> p b n"),
+            )
+            x_tiles.extend([x_tile[:, image, :, :] for image in range(images)])
             if r == 0:
                 for quadrant in range(QUADRANTS):
                     nc.sync.dma_start(

@@ -20,6 +20,7 @@ HW = 256
 QUADRANTS = 4
 GP_POS = 192
 HEAD_ROUNDS = 2
+FIRST_VECTOR_POS = 144
 HEAD_COPY_POS = 128
 
 FLOPS = 2 * BATCH * HW * BLOCKS * CD * CD
@@ -39,8 +40,10 @@ def tile_spectralchannelmixing_e_kernel(tc, x, wc_words, wc_scales, out):
         psum = ctx.enter_context(tc.psum_pool(name="psum", bufs=6))
         psum_grp = ctx.enter_context(tc.psum_pool(name="psum_grp", bufs=2))
 
-        scales_raw = const.tile([P, BLOCKS, CD], U8, align_bytes=64)
+        scales_raw = const.tile([P, CD], U8, align_bytes=64)
         nc.vector.memset(scales_raw[:].bitcast(I32), 0)
+        later_scales = const.tile([P, BLOCKS - 1, PACK, P], U8, align_bytes=64)
+        nc.vector.memset(later_scales[:].rearrange("p g t m -> p (g t m)").bitcast(I32), 0)
         zero = const.tile([P, 1], F32)
         nc.vector.memset(zero[:], 0.0)
         warm = const.tile([P, 1], F32)
@@ -51,33 +54,36 @@ def tile_spectralchannelmixing_e_kernel(tc, x, wc_words, wc_scales, out):
 
         words_raw = const.tile([P, BLOCKS, 2 * CD], U8, align_bytes=64)
         x_tiles = []
-        nc.sync.dma_start(
-            out=words_raw[:].bitcast(I32), in_=wc_words.bitcast(I32).rearrange("g p n -> p g n")
-        )
-        for r, (i, b) in enumerate(rounds):
-            if r < 2:
-                images = 1
-            elif r % 2 == 0:
-                images = 2
-            else:
-                continue
+        nc.sync.dma_start(out=words_raw[:, 0, :].bitcast(I32), in_=wc_words[0].bitcast(I32))
+
+        def load_images(r, images):
+            i, b = rounds[r]
             x_tile = const.tile([P, images, PACK, HW], BF16, name="x_tile%d" % r)
             nc.sync.dma_start(
                 out=x_tile[:].rearrange("p b t s -> p b (t s)"),
                 in_=x_view[i, b : b + images].rearrange("b p n -> p b n"),
             )
             x_tiles.extend([x_tile[:, image, :, :] for image in range(images)])
-            if r == 0:
-                for quadrant in range(QUADRANTS):
-                    nc.sync.dma_start(
-                        out=scales_raw[32 * quadrant : 32 * quadrant + 4, :, :].bitcast(I32),
-                        in_=wc_scales.bitcast(I32)[
-                            :, 4 * quadrant : 4 * quadrant + 4, :
-                        ].rearrange("g r n -> r g n"),
-                    )
+
+        def load_scales():
+            for quadrant in range(QUADRANTS):
+                nc.sync.dma_start(
+                    out=scales_raw[32 * quadrant : 32 * quadrant + 16, :].bitcast(I32),
+                    in_=wc_scales.bitcast(I32)[:, 4 * quadrant : 4 * quadrant + 4, :],
+                )
+
+        load_images(0, 1)
+        load_scales()
+        nc.sync.dma_start(
+            out=words_raw[:, 1:BLOCKS, :].bitcast(I32),
+            in_=wc_words.bitcast(I32)[1:BLOCKS].rearrange("g p n -> p g n"),
+        )
+        load_images(1, 1)
+        for r in (2, 4, 6):
+            load_images(r, 2)
 
         words_sorted = const.tile([P, BLOCKS, PACK, 2 * P], U8, align_bytes=64)
-        scales_sorted = const.tile([P, BLOCKS, PACK, P], U8, align_bytes=64)
+        scales_sorted = const.tile([P, PACK, P], U8, align_bytes=64)
 
         def sort_words(i):
             nc.vector.tensor_copy(
@@ -85,11 +91,22 @@ def tile_spectralchannelmixing_e_kernel(tc, x, wc_words, wc_scales, out):
                 in_=words_raw[:, i, :].rearrange("p (m t e) -> p t m e", t=PACK, e=2),
             )
 
-        def sort_scales(i):
+        def sort_scales():
             nc.vector.tensor_copy(
-                out=scales_sorted[:, i, :, :],
-                in_=scales_raw[:, i, :].rearrange("p (m t) -> p t m", t=PACK),
+                out=scales_sorted[:], in_=scales_raw[:].rearrange("p (m t) -> p t m", t=PACK)
             )
+
+        def move_scales(i):
+            for quadrant in range(QUADRANTS):
+                first_row = 32 * quadrant
+                nc.sync.dma_start(
+                    out=later_scales[first_row : first_row + 4, i - 1, :, :]
+                    .rearrange("p t m -> p (t m)")
+                    .bitcast(I32),
+                    in_=scales_sorted[first_row + 4 * i : first_row + 4 * i + 4, :, :]
+                    .rearrange("p t m -> p (t m)")
+                    .bitcast(I32),
+                )
 
         grouped, x_codes, x_scales = {}, {}, {}
         banks, sums = {}, {}
@@ -98,6 +115,16 @@ def tile_spectralchannelmixing_e_kernel(tc, x, wc_words, wc_scales, out):
             grouped[r] = stage.tile([P, HW, PACK], BF16, align_bytes=64, name="grouped")
             head = r < HEAD_ROUNDS
             first = HEAD_COPY_POS if head else GP_POS
+            if r == 0:
+                nc.vector.tensor_copy(
+                    out=grouped[r][:, 0:FIRST_VECTOR_POS, :],
+                    in_=x_tiles[r][:, :, 0:FIRST_VECTOR_POS].rearrange("p t s -> p s t"),
+                )
+                nc.scalar.copy(
+                    out=grouped[r][:, FIRST_VECTOR_POS:HW, :],
+                    in_=x_tiles[r][:, :, FIRST_VECTOR_POS:HW].rearrange("p t s -> p s t"),
+                )
+                return
             if head:
                 nc.scalar.copy(
                     out=grouped[r][:, 0:first, :],
@@ -140,46 +167,71 @@ def tile_spectralchannelmixing_e_kernel(tc, x, wc_words, wc_scales, out):
                     nc.tensor.matmul_mx(
                         out=banks[r, h][:, e, :],
                         lhsT=words_sorted[:, i, t, :].bitcast(FP4X4),
-                        lhsT_scale=scales_sorted[:, i, t, :],
+                        lhsT_scale=scales_sorted[:, t, :] if i == 0 else later_scales[:, i - 1, t, :],
                         rhs=x_codes[r][:].bitcast(FP8X4),
                         rhs_scale=x_scales[r][:],
                         start=True,
                         stop=True,
                     )
 
+        def piece_width(r):
+            return 1 if r == len(rounds) - 1 else 2
+
         def add_residual(r):
             sums[r] = stage.tile([P, PACK, HW], F32, name="sums")
-            for h in range(2):
+            width = piece_width(r)
+            for t in range(0, PACK, width):
                 nc.vector.tensor_tensor(
-                    out=sums[r][:, 2 * h : 2 * h + 2, :],
-                    in0=banks[r, h][:],
-                    in1=x_tiles[r][:, 2 * h : 2 * h + 2, :],
+                    out=sums[r][:, t : t + width, :],
+                    in0=banks[r, t // 2][:, t % 2 : t % 2 + width, :],
+                    in1=x_tiles[r][:, t : t + width, :],
                     op=mybir.AluOpType.add,
                 )
 
         def gelu_and_store(r):
             i, b = rounds[r]
             result = results.tile([P, PACK, HW], F32, name="result")
-            for h in range(2):
+            width = piece_width(r)
+            for t in range(0, PACK, width):
                 nc.scalar.activation(
-                    out=result[:, 2 * h : 2 * h + 2, :],
-                    in_=sums[r][:, 2 * h : 2 * h + 2, :],
+                    out=result[:, t : t + width, :],
+                    in_=sums[r][:, t : t + width, :],
                     func=mybir.ActivationFunctionType.Gelu,
                 )
-            nc.sync.dma_start(out=out_view[i, b], in_=result[:].rearrange("p t s -> p (t s)"))
+                if r >= len(rounds) - 2:
+                    nc.sync.dma_start(
+                        out=out_view[i, b][:, t * HW : (t + width) * HW],
+                        in_=result[:, t : t + width, :].rearrange("p t s -> p (t s)"),
+                    )
+            if r < len(rounds) - 2:
+                nc.sync.dma_start(out=out_view[i, b], in_=result[:].rearrange("p t s -> p (t s)"))
 
         def at(r, stage_of_round):
             if 0 <= r < len(rounds):
                 stage_of_round(r)
 
-        for i in range(BLOCKS):
+        sort_words(0)
+        regroup(0)
+        quantise(0)
+        sort_scales()
+        move_scales(1)
+        load_images(8, 2)
+        load_images(10, 2)
+        move_scales(2)
+        load_images(12, 2)
+        load_images(14, 2)
+        move_scales(3)
+        regroup(1)
+        multiply(0)
+        for i in range(1, BLOCKS):
             sort_words(i)
-        sort_scales(0)
-        for k in range(-3, len(rounds) + 1):
+        regroup(2)
+        quantise(1)
+        add_residual(0)
+        regroup(3)
+        for k in range(1, len(rounds) + 1):
             at(k, multiply)
             at(k + 1, quantise)
             at(k, add_residual)
-            if k >= 0 and k % BATCH == 1 and k // BATCH + 1 < BLOCKS:
-                sort_scales(k // BATCH + 1)
             at(k - 1, gelu_and_store)
             at(k + 3, regroup)

@@ -18,7 +18,7 @@ BLOCKS = 4
 CD = P * PACK
 HW = 256
 QUADRANTS = 4
-GP_POS = 192
+GP_POS = 176
 HEAD_ROUNDS = 2
 FIRST_VECTOR_POS = 144
 HEAD_COPY_POS = 128

from contextlib import ExitStack

import concourse.mybir as mybir
from concourse.masks import make_identity

BF16 = mybir.dt.bfloat16
F32 = mybir.dt.float32
I32 = mybir.dt.int32
U8 = mybir.dt.uint8
U32 = mybir.dt.uint32
FP8X4 = mybir.dt.float8_e4m3fn_x4
FP4X4 = mybir.dt.float4_e2m1fn_x4

P = 128
PACK = 4
BATCH = 4
BLOCKS = 4
CD = P * PACK
HW = 256
QUADRANTS = 4
GP_POS = 176
HEAD_ROUNDS = 2
FIRST_VECTOR_POS = 144
HEAD_COPY_POS = 128

FLOPS = 2 * BATCH * HW * BLOCKS * CD * CD


def tile_spectralchannelmixing_e_kernel(tc, x, wc_words, wc_scales, out):
    nc = tc.nc
    x_view = x.rearrange("b (i p t) h w -> i b p (t h w)", i=BLOCKS, t=PACK)
    out_view = out.rearrange("b (i p t) h w -> i b p (t h w)", i=BLOCKS, t=PACK)
    rounds = [(i, b) for i in range(BLOCKS) for b in range(BATCH)]

    with ExitStack() as ctx:
        ctx.enter_context(tc.manual_schedule())
        const = ctx.enter_context(tc.tile_pool(name="const", bufs=1))
        stage = ctx.enter_context(tc.tile_pool(name="stage", bufs=4))
        results = ctx.enter_context(tc.tile_pool(name="results", bufs=6))
        psum = ctx.enter_context(tc.psum_pool(name="psum", bufs=6))
        psum_grp = ctx.enter_context(tc.psum_pool(name="psum_grp", bufs=2))

        scales_raw = const.tile([P, CD], U8, align_bytes=64)
        nc.vector.memset(scales_raw[:].bitcast(I32), 0)
        later_scales = const.tile([P, BLOCKS - 1, PACK, P], U8, align_bytes=64)
        nc.vector.memset(later_scales[:].rearrange("p g t m -> p (g t m)").bitcast(I32), 0)
        zero = const.tile([P, 1], F32)
        nc.vector.memset(zero[:], 0.0)
        warm = const.tile([P, 1], F32)
        nc.scalar.activation(out=warm[:], in_=zero[:], func=mybir.ActivationFunctionType.Gelu)

        ident = const.tile([P, P], BF16)
        make_identity(nc, ident[:])

        words_raw = const.tile([P, BLOCKS, 2 * CD], U8, align_bytes=64)
        x_tiles = []
        nc.sync.dma_start(out=words_raw[:, 0, :].bitcast(I32), in_=wc_words[0].bitcast(I32))

        def load_images(r, images):
            i, b = rounds[r]
            x_tile = const.tile([P, images, PACK, HW], BF16, name="x_tile%d" % r)
            nc.sync.dma_start(
                out=x_tile[:].rearrange("p b t s -> p b (t s)"),
                in_=x_view[i, b : b + images].rearrange("b p n -> p b n"),
            )
            x_tiles.extend([x_tile[:, image, :, :] for image in range(images)])

        def load_scales():
            for quadrant in range(QUADRANTS):
                nc.sync.dma_start(
                    out=scales_raw[32 * quadrant : 32 * quadrant + 16, :].bitcast(I32),
                    in_=wc_scales.bitcast(I32)[:, 4 * quadrant : 4 * quadrant + 4, :],
                )

        load_images(0, 1)
        load_scales()
        nc.sync.dma_start(
            out=words_raw[:, 1:BLOCKS, :].bitcast(I32),
            in_=wc_words.bitcast(I32)[1:BLOCKS].rearrange("g p n -> p g n"),
        )
        load_images(1, 1)
        for r in (2, 4, 6):
            load_images(r, 2)

        words_sorted = const.tile([P, BLOCKS, PACK, 2 * P], U8, align_bytes=64)
        scales_sorted = const.tile([P, PACK, P], U8, align_bytes=64)

        def sort_words(i):
            nc.vector.tensor_copy(
                out=words_sorted[:, i, :, :].rearrange("p t (m e) -> p t m e", e=2),
                in_=words_raw[:, i, :].rearrange("p (m t e) -> p t m e", t=PACK, e=2),
            )

        def sort_scales():
            nc.vector.tensor_copy(
                out=scales_sorted[:], in_=scales_raw[:].rearrange("p (m t) -> p t m", t=PACK)
            )

        def move_scales(i):
            for quadrant in range(QUADRANTS):
                first_row = 32 * quadrant
                nc.sync.dma_start(
                    out=later_scales[first_row : first_row + 4, i - 1, :, :]
                    .rearrange("p t m -> p (t m)")
                    .bitcast(I32),
                    in_=scales_sorted[first_row + 4 * i : first_row + 4 * i + 4, :, :]
                    .rearrange("p t m -> p (t m)")
                    .bitcast(I32),
                )

        grouped, x_codes, x_scales = {}, {}, {}
        banks, sums = {}, {}

        def regroup(r):
            grouped[r] = stage.tile([P, HW, PACK], BF16, align_bytes=64, name="grouped")
            head = r < HEAD_ROUNDS
            first = HEAD_COPY_POS if head else GP_POS
            if r == 0:
                nc.vector.tensor_copy(
                    out=grouped[r][:, 0:FIRST_VECTOR_POS, :],
                    in_=x_tiles[r][:, :, 0:FIRST_VECTOR_POS].rearrange("p t s -> p s t"),
                )
                nc.scalar.copy(
                    out=grouped[r][:, FIRST_VECTOR_POS:HW, :],
                    in_=x_tiles[r][:, :, FIRST_VECTOR_POS:HW].rearrange("p t s -> p s t"),
                )
                return
            if head:
                nc.scalar.copy(
                    out=grouped[r][:, 0:first, :],
                    in_=x_tiles[r][:, :, 0:first].rearrange("p t s -> p s t"),
                )
            else:
                nc.gpsimd.tensor_scalar(
                    out=grouped[r][:, 0:first, :],
                    in0=x_tiles[r][:, :, 0:first].rearrange("p t s -> p s t"),
                    scalar1=1.0,
                    scalar2=0.0,
                    op0=mybir.AluOpType.mult,
                    op1=mybir.AluOpType.add,
                )
            grp_bank = psum_grp.tile([P, HW - first, PACK], BF16, name="grp_bank")
            nc.tensor.matmul(
                out=grp_bank[:],
                lhsT=ident[:],
                rhs=x_tiles[r][:, :, first:HW].rearrange("p t s -> p s t"),
                start=True,
                stop=True,
            )
            nc.scalar.copy(out=grouped[r][:, first:HW, :], in_=grp_bank[:])

        def quantise(r):
            x_codes[r] = stage.tile([P, HW], U32, align_bytes=64, name="x_codes")
            x_scales[r] = stage.tile([P, HW], U8, align_bytes=64, name="x_scales")
            nc.vector.quantize_mx(
                out=x_codes[r][:].bitcast(FP8X4),
                scales=x_scales[r][:],
                in_=grouped[r][:].rearrange("p s t -> p (s t)"),
            )

        def multiply(r):
            i = rounds[r][0]
            for h in range(2):
                banks[r, h] = psum.tile([P, 2, HW], F32, name="bank")
                for e in range(2):
                    t = 2 * h + e
                    nc.tensor.matmul_mx(
                        out=banks[r, h][:, e, :],
                        lhsT=words_sorted[:, i, t, :].bitcast(FP4X4),
                        lhsT_scale=scales_sorted[:, t, :] if i == 0 else later_scales[:, i - 1, t, :],
                        rhs=x_codes[r][:].bitcast(FP8X4),
                        rhs_scale=x_scales[r][:],
                        start=True,
                        stop=True,
                    )

        def piece_width(r):
            return 1 if r == len(rounds) - 1 else 2

        def add_residual(r):
            sums[r] = stage.tile([P, PACK, HW], F32, name="sums")
            width = piece_width(r)
            for t in range(0, PACK, width):
                nc.vector.tensor_tensor(
                    out=sums[r][:, t : t + width, :],
                    in0=banks[r, t // 2][:, t % 2 : t % 2 + width, :],
                    in1=x_tiles[r][:, t : t + width, :],
                    op=mybir.AluOpType.add,
                )

        def gelu_and_store(r):
            i, b = rounds[r]
            result = results.tile([P, PACK, HW], F32, name="result")
            width = piece_width(r)
            for t in range(0, PACK, width):
                nc.scalar.activation(
                    out=result[:, t : t + width, :],
                    in_=sums[r][:, t : t + width, :],
                    func=mybir.ActivationFunctionType.Gelu,
                )
                if r >= len(rounds) - 2:
                    nc.sync.dma_start(
                        out=out_view[i, b][:, t * HW : (t + width) * HW],
                        in_=result[:, t : t + width, :].rearrange("p t s -> p (t s)"),
                    )
            if r < len(rounds) - 2:
                nc.sync.dma_start(out=out_view[i, b], in_=result[:].rearrange("p t s -> p (t s)"))

        def at(r, stage_of_round):
            if 0 <= r < len(rounds):
                stage_of_round(r)

        sort_words(0)
        regroup(0)
        quantise(0)
        sort_scales()
        move_scales(1)
        load_images(8, 2)
        load_images(10, 2)
        move_scales(2)
        load_images(12, 2)
        load_images(14, 2)
        move_scales(3)
        regroup(1)
        multiply(0)
        for i in range(1, BLOCKS):
            sort_words(i)
        regroup(2)
        quantise(1)
        add_residual(0)
        regroup(3)
        for k in range(1, len(rounds) + 1):
            at(k, multiply)
            at(k + 1, quantise)
            at(k, add_residual)
            at(k - 1, gelu_and_store)
            at(k + 3, regroup)
